import numpy as np
import ml_dtypes


def mxq(x, axis, fmt="e4m3"):
    dtype, down = {"e4m3": (ml_dtypes.float8_e4m3fn, 7), "e5m2": (ml_dtypes.float8_e5m2, 14)}[fmt]
    v = np.moveaxis(np.asarray(x, np.float32).astype(ml_dtypes.bfloat16).astype(np.float64), axis, -1)
    blocks = v.reshape(v.shape[:-1] + (-1, 32))
    amax = np.abs(blocks).max(-1, keepdims=True)
    byte = np.maximum(np.where(amax > 0, np.frexp(amax)[1] - 1 + 127, 0) - down, 1)
    scale = np.exp2(byte - 127.0)
    codes = (blocks / scale).astype(np.float32).astype(dtype).astype(np.float64)
    return np.moveaxis((codes * scale).reshape(v.shape), -1, axis)


WIDE = False


def mx_kscale(k):
    if not WIDE:
        return np.ones(k)
    levels = np.array([10, -10, 5, -5, 0])
    a = np.random.permutation(np.resize(levels, k // 512 * 4)).reshape(k // 512, 4)
    idx = np.arange(k)
    return np.exp2(a[idx // 512, idx % 128 // 32])


BF16 = ml_dtypes.bfloat16


def bf(x):
    return np.asarray(x, np.float32).astype(BF16)


def f64(x):
    return np.asarray(x).astype(np.float64)


B, IN, NLVL, KLVL, C, CM, CO, OU, OV = 8, 256, 6, 3, 128, 128, 128, 8, 8
P = 2 ** (KLVL - 2)
S = 2 ** (NLVL - KLVL + 2)
KA, KB = 4 * C, 4 * CM


def patches(x):
    U, V, Bn, H, W, Cc = x.shape
    return x.reshape(U, V, Bn, H // 2, 2, W // 2, 2, Cc).swapaxes(4, 5).reshape(U, V, Bn * (H // 2) * (W // 2), 4 * Cc)


def branch_conv(x, w, b):
    U, V, Bn, H, W, Cc = x.shape
    Co = w.shape[-1]
    R = Bn * (H // 2) * (W // 2)
    p = patches(x).reshape(U, 1, V, 1, R, 4 * Cc)
    wc = w.reshape(U, 2, V, 2, 4 * Cc, Co)
    y = (mxq(p, 5, "e4m3") @ mxq(wc, 4, "e4m3")) + b.reshape(U, 2, V, 2, 1, Co)
    return np.maximum(y, 0.0).reshape(2 * U, 2 * V, Bn, H // 2, W // 2, Co)


def setup_inputs():
    s = mx_kscale(KA).reshape(2, 2, C)
    t = mx_kscale(KB)[:CM]
    x = np.maximum(np.random.standard_normal((P, P, B, S, S, C)), 0.0) * np.tile(s, (S // 2, S // 2, 1))
    return {"x_parent": bf(x),
            "f_child": bf(np.random.standard_normal((2 * P, 2 * P, 2, 2, C, CM)) * np.sqrt(0.5 / C) / s[:, :, :, None] * t),
            "b_child": bf(np.random.standard_normal((2 * P, 2 * P, CM)) * 0.2 * t),
            "f_gchild": bf(np.random.standard_normal((4 * P, 4 * P, 2, 2, CM, CO)) * np.sqrt(0.5 / CM) / t[:, None]),
            "b_gchild": bf(np.random.standard_normal((4 * P, 4 * P, CO)) * 0.2)}


def reference(x_parent, f_child, b_child, f_gchild, b_gchild):
    h = branch_conv(f64(x_parent), f64(f_child), f64(b_child))
    return branch_conv(h, f64(f_gchild), f64(b_gchild))

@@ -1,0 +1,247 @@
+from contextlib import ExitStack
+
+import concourse.mybir as mybir
+from concourse.masks import make_identity
+
+F32 = mybir.dt.float32
+BF16 = mybir.dt.bfloat16
+U32 = mybir.dt.uint32
+U8 = mybir.dt.uint8
+FP8X4 = mybir.dt.float8_e4m3fn_x4
+
+P = 128
+PACK = 4
+N_COLS = 512
+GROUP = PACK * N_COLS
+CHUNKS = 4
+PARENTS = 4
+CHILDREN = 16
+GRANDCHILDREN = 64
+X_ROW = 2 * 32 * P
+
+FLOPS = 2 * 512 * P * (CHILDREN * 2048 + GRANDCHILDREN * 512)
+
+
+def tile_butterflylayer2d_pa_kernel(tc, x_parent, f_child, b_child, f_gchild, b_gchild, out):
+    nc = tc.nc
+    relu = mybir.ActivationFunctionType.Relu
+    add = mybir.AluOpType.add
+
+    x_view = x_parent.rearrange("u v n (y p) w c -> (u v) (n y) (p w c)", p=2)
+    fc_view = f_child.rearrange("i j p q (cw e) o -> (q cw) i (j p) (e o)", e=2)
+    fg_view = f_gchild.rearrange("i j p q c o -> c i (j p q) o")
+    out_view = out.rearrange("i j n y (hi lo) o -> i (n y hi) j (lo o)", hi=2)
+
+    children = []
+    for u in range(2):
+        for v in range(2):
+            for a in range(2):
+                for e in range(2):
+                    children.append((2 * u + a, 2 * v + e))
+
+    with ExitStack() as ctx:
+        const = ctx.enter_context(tc.tile_pool(name="const", bufs=1))
+        x_pool = ctx.enter_context(tc.tile_pool(name="x", bufs=2))
+        raw_pool = ctx.enter_context(tc.tile_pool(name="raw", bufs=4))
+        group_pool = ctx.enter_context(tc.tile_pool(name="group", bufs=3))
+        x_code_pool = ctx.enter_context(tc.tile_pool(name="xcode", bufs=2))
+        code_pool = ctx.enter_context(tc.tile_pool(name="code", bufs=3))
+        out_pool = ctx.enter_context(tc.tile_pool(name="outs", bufs=3))
+        psum_t = ctx.enter_context(tc.psum_pool(name="psum_t", bufs=2))
+        psum_h = ctx.enter_context(tc.psum_pool(name="psum_h", bufs=3))
+        psum_o = ctx.enter_context(tc.psum_pool(name="psum_o", bufs=3))
+
+        x_tiles = {}
+        fc_raws = {}
+        x_codes = {}
+        fg_raws = {}
+        fg_codes = {}
+        h_codes = {}
+
+        def load_x(parent):
+            x_sb = x_pool.tile([P, X_ROW], BF16)
+            nc.sync.dma_start(out=x_sb[:], in_=x_view[parent])
+            x_tiles[parent] = x_sb
+
+        def load_fg(step):
+            ci, cj = children[step]
+            fg_raw = raw_pool.tile([P, GROUP], BF16)
+            for a in range(2):
+                nc.sync.dma_start(
+                    out=fg_raw[:, a * 1024 : (a + 1) * 1024].rearrange("k (r o) -> k r o", o=P),
+                    in_=fg_view[:, 2 * ci + a, 8 * cj : 8 * cj + 8, :],
+                )
+            fg_raws[step] = fg_raw
+
+        def quantise_weights(raw, codes, scales):
+            grouped = group_pool.tile([P, GROUP], BF16, align_bytes=64, tag="w_grouped")
+            nc.vector.tensor_copy(
+                out=grouped[:].rearrange("k (g o t) -> k g o t", g=4, t=PACK),
+                in_=raw[:].rearrange("k (g t o) -> k g o t", g=4, t=PACK),
+            )
+            nc.vector.quantize_mx(out=codes.bitcast(FP8X4), scales=scales, in_=grouped[:])
+
+        fc_codes = const.tile([P, 4, N_COLS], U32, align_bytes=64)
+        fc_scales = const.tile([P, 4, N_COLS], U8, align_bytes=64)
+
+        def load_fc(i):
+            fc_raw = raw_pool.tile([P, GROUP], BF16)
+            nc.sync.dma_start(out=fc_raw[:].rearrange("k (r w) -> k r w", w=2 * P), in_=fc_view[:, i])
+            fc_raws[i] = fc_raw
+
+        def quantise_fc(i):
+            quantise_weights(fc_raws[i], fc_codes[:, i, :], fc_scales[:, i, :])
+
+        def quantise_fg(step):
+            fg_code = code_pool.tile([P, N_COLS], U32, align_bytes=64)
+            fg_scale = code_pool.tile([P, N_COLS], U8, align_bytes=64)
+            quantise_weights(fg_raws[step], fg_code[:], fg_scale[:])
+            fg_codes[step] = (fg_code, fg_scale)
+
+        def new_x_codes(parent):
+            x_code = x_code_pool.tile([P, CHUNKS, N_COLS], U32, align_bytes=64)
+            x_scale = x_code_pool.tile([P, CHUNKS, N_COLS], U8, align_bytes=64)
+            x_codes[parent] = (x_code, x_scale)
+
+        def quantise_patches(parent, chunk):
+            x_words = x_tiles[parent][:].bitcast(F32)
+            x_code, x_scale = x_codes[parent]
+            patches = group_pool.tile([P, GROUP], BF16, align_bytes=64)
+            patch_words = patches[:].bitcast(F32).rearrange("k (hi r t) -> k hi r t", hi=2, t=PACK)
+            for hi in range(2):
+                flipped = psum_t.tile([P, PACK, P], F32)
+                for x_low in range(2):
+                    for p in range(2):
+                        x = 2 * (4 * hi + chunk) + x_low
+                        first = p * (X_ROW // 4) + x * P
+                        nc.tensor.transpose(flipped[:, 2 * x_low + p, :], x_words[:, first : first + P], ident_f32[:])
+                nc.scalar.copy(out=patch_words[:, hi], in_=flipped[:].rearrange("k t r -> k r t"))
+            nc.vector.quantize_mx(out=x_code[:, chunk, :].bitcast(FP8X4), scales=x_scale[:, chunk, :], in_=patches[:])
+
+        def level_1(step):
+            ci, cj = children[step]
+            x_code, x_scale = x_codes[step // 4]
+            h_bf = group_pool.tile([P, GROUP], BF16, align_bytes=64)
+            for chunk in range(CHUNKS):
+                h_ps = psum_h.tile([P, N_COLS], F32)
+                nc.tensor.matmul_mx(
+                    out=h_ps[:],
+                    lhsT=fc_codes[:, ci, cj * P : (cj + 1) * P].bitcast(FP8X4),
+                    lhsT_scale=fc_scales[:, ci, cj * P : (cj + 1) * P],
+                    rhs=x_code[:, chunk, :].bitcast(FP8X4),
+                    rhs_scale=x_scale[:, chunk, :],
+                    start=True,
+                    stop=True,
+                )
+                nc.scalar.activation(
+                    out=h_bf[:, chunk * N_COLS : (chunk + 1) * N_COLS].rearrange("k (r hi t) -> k r hi t", hi=2, t=PACK),
+                    in_=h_ps[:].rearrange("k (hi r t) -> k r hi t", hi=2, t=PACK),
+                    func=relu,
+                    bias=bias_cols[:, 4 * ci + cj : 4 * ci + cj + 1],
+                    scale=1.0,
+                )
+            h_code = code_pool.tile([P, N_COLS], U32, align_bytes=64)
+            h_scale = code_pool.tile([P, N_COLS], U8, align_bytes=64)
+            nc.vector.quantize_mx(out=h_code[:].bitcast(FP8X4), scales=h_scale[:], in_=h_bf[:])
+            h_codes[step] = (h_code, h_scale)
+
+        def level_2(step):
+            ci, cj = children[step]
+            h_code, h_scale = h_codes[step]
+            fg_code, fg_scale = fg_codes[step]
+            out_sb = out_pool.tile([P, 4, CHUNKS, P], F32)
+            for chunk in range(CHUNKS):
+                o_ps = psum_o.tile([P, N_COLS], F32)
+                nc.tensor.matmul_mx(
+                    out=o_ps[:],
+                    lhsT=h_code[:, chunk * P : (chunk + 1) * P].bitcast(FP8X4),
+                    lhsT_scale=h_scale[:, chunk * P : (chunk + 1) * P],
+                    rhs=fg_code[:].bitcast(FP8X4),
+                    rhs_scale=fg_scale[:],
+                    start=True,
+                    stop=True,
+                )
+                nc.vector.tensor_tensor(
+                    out=out_sb[:, :, chunk, :].rearrange("k (a e) o -> k a e o", a=2),
+                    in0=o_ps[:].rearrange("k (a e o) -> k a e o", a=2, e=2),
+                    in1=bias_spread[:, 2 * ci : 2 * ci + 2, 2 * cj : 2 * cj + 2, :],
+                    op=add,
+                )
+            flat = out_sb[:].rearrange("k g lo o -> k (g lo o)")
+            nc.scalar.activation(out=flat, in_=flat, func=relu)
+            for a in range(2):
+                nc.scalar.dma_start(
+                    out=out_view[2 * ci + a, :, 2 * cj : 2 * cj + 2, :],
+                    in_=out_sb[:, 2 * a : 2 * a + 2, :, :].rearrange("k e lo o -> k e (lo o)"),
+                )
+
+        bias_rows = const.tile([P, P], BF16)
+        nc.vector.memset(bias_rows[:], 0.0)
+        nc.sync.dma_start(out=bias_rows[0:CHILDREN, :], in_=b_child.rearrange("i j o -> (i j) o"))
+        nc.sync.dma_start(
+            out=bias_rows[CHILDREN : CHILDREN + GRANDCHILDREN, :], in_=b_gchild.rearrange("i j o -> (i j) o")
+        )
+        load_fc(0)
+        load_x(0)
+        load_fc(1)
+        load_fg(0)
+        load_fg(1)
+        load_x(1)
+
+        ident_bf = const.tile([P, P], BF16)
+        make_identity(nc, ident_bf[:])
+        ident_f32 = const.tile([P, P], F32)
+        make_identity(nc, ident_f32[:])
+
+        bias_ps = psum_t.tile([P, P], BF16, tag="flipped")
+        nc.tensor.transpose(bias_ps[:], bias_rows[:], ident_bf[:])
+        bias_cols = const.tile([P, P], F32)
+        nc.vector.tensor_copy(out=bias_cols[:], in_=bias_ps[:])
+        bias_cols_bf = const.tile([P, P], BF16)
+        nc.vector.tensor_copy(out=bias_cols_bf[:], in_=bias_ps[:])
+        bias_spread = const.tile([P, 8, 8, P], BF16)
+        for i in range(8):
+            for half in range(2):
+                spread_ps = psum_o.tile([P, 4, P], F32, tag="o_ps")
+                for j in range(4):
+                    node = CHILDREN + 8 * i + 4 * half + j
+                    nc.tensor.matmul(
+                        out=spread_ps[:, j, :],
+                        lhsT=bias_cols_bf[:, node : node + 1].to_broadcast([P, P]),
+                        rhs=ident_bf[:],
+                        start=True,
+                        stop=True,
+                    )
+                if half == 0:
+                    nc.vector.tensor_copy(out=bias_spread[:, i, 0:4, :], in_=spread_ps[:])
+                else:
+                    nc.scalar.copy(out=bias_spread[:, i, 4:8, :], in_=spread_ps[:])
+
+        quantise_fc(0)
+        new_x_codes(0)
+        for chunk in range(CHUNKS):
+            quantise_patches(0, chunk)
+        quantise_fc(1)
+        quantise_fg(0)
+
+        for step in range(CHILDREN):
+            parent = step // 4
+            chunk = step % 4
+            if step + 2 < CHILDREN:
+                load_fg(step + 2)
+            if chunk == 0 and parent + 2 < PARENTS:
+                load_x(parent + 2)
+            if step < 2:
+                load_fc(step + 2)
+            elif step < 4:
+                quantise_fc(step)
+            if step + 1 < CHILDREN:
+                quantise_fg(step + 1)
+            if parent + 1 < PARENTS:
+                if chunk == 0:
+                    new_x_codes(parent + 1)
+                quantise_patches(parent + 1, chunk)
+            level_1(step)
+            if step > 0:
+                level_2(step - 1)
+        level_2(CHILDREN - 1)

@@ -17,17 +17,28 @@ CHUNKS = 4
 PARENTS = 4
 CHILDREN = 16
 GRANDCHILDREN = 64
-X_ROW = 2 * 32 * P
+
+X_LOAD_LEAD = 7
+FLIP_LEAD = 4
+LEVEL_2_LAG = 2
+FINISH_LAG = 3
+FG_LOAD_LEAD = 4
+REGROUP_LEAD = 2
 
 FLOPS = 2 * 512 * P * (CHILDREN * 2048 + GRANDCHILDREN * 512)
+
+
+def live(index, count):
+    return 0 <= index < count
 
 
 def tile_butterflylayer2d_pa_kernel(tc, x_parent, f_child, b_child, f_gchild, b_gchild, out):
     nc = tc.nc
     relu = mybir.ActivationFunctionType.Relu
     add = mybir.AluOpType.add
+    mult = mybir.AluOpType.mult
 
-    x_view = x_parent.rearrange("u v n (y p) w c -> (u v) (n y) (p w c)", p=2)
+    x_view = x_parent.rearrange("u v n (y p) (hi lo w) c -> (u v) lo (n y) (p hi) (w c)", p=2, hi=2, lo=CHUNKS)
     fc_view = f_child.rearrange("i j p q (cw e) o -> (q cw) i (j p) (e o)", e=2)
     fg_view = f_gchild.rearrange("i j p q c o -> c i (j p q) o")
     out_view = out.rearrange("i j n y (hi lo) o -> i (n y hi) j (lo o)", hi=2)
@@ -41,139 +52,170 @@ def tile_butterflylayer2d_pa_kernel(tc, x_parent, f_child, b_child, f_gchild, b_
 
     with ExitStack() as ctx:
         const = ctx.enter_context(tc.tile_pool(name="const", bufs=1))
-        x_pool = ctx.enter_context(tc.tile_pool(name="x", bufs=2))
-        raw_pool = ctx.enter_context(tc.tile_pool(name="raw", bufs=4))
-        group_pool = ctx.enter_context(tc.tile_pool(name="group", bufs=3))
+        x_pool = ctx.enter_context(tc.tile_pool(name="x", bufs=5))
+        fc_pool = ctx.enter_context(tc.tile_pool(name="fc", bufs=4))
+        fg_pool = ctx.enter_context(tc.tile_pool(name="fg", bufs=6))
+        group_pool = ctx.enter_context(tc.tile_pool(name="group", bufs=2))
         x_code_pool = ctx.enter_context(tc.tile_pool(name="xcode", bufs=2))
         code_pool = ctx.enter_context(tc.tile_pool(name="code", bufs=3))
-        out_pool = ctx.enter_context(tc.tile_pool(name="outs", bufs=3))
+        out_pool = ctx.enter_context(tc.tile_pool(name="outs", bufs=4))
         psum_t = ctx.enter_context(tc.psum_pool(name="psum_t", bufs=2))
         psum_h = ctx.enter_context(tc.psum_pool(name="psum_h", bufs=3))
         psum_o = ctx.enter_context(tc.psum_pool(name="psum_o", bufs=3))
+        ctx.enter_context(tc.manual_schedule())
 
         x_tiles = {}
-        fc_raws = {}
         x_codes = {}
+        patch_tiles = {}
+        fc_raws = {}
+        fc_groups = {}
         fg_raws = {}
+        fg_groups = {}
         fg_codes = {}
+        h_tiles = {}
         h_codes = {}
+        out_tiles = {}
 
-        def load_x(parent):
-            x_sb = x_pool.tile([P, X_ROW], BF16)
-            nc.sync.dma_start(out=x_sb[:], in_=x_view[parent])
-            x_tiles[parent] = x_sb
+        def load_x(parent, chunk):
+            x_sb = x_pool.tile([P, GROUP], BF16)
+            nc.sync.dma_start(out=x_sb[:].rearrange("k (s r) -> k s r", s=PACK), in_=x_view[parent, chunk])
+            x_tiles[(parent, chunk)] = x_sb
 
-        def load_fg(step):
-            ci, cj = children[step]
-            fg_raw = raw_pool.tile([P, GROUP], BF16)
+        def load_fc(i):
+            fc_raw = fc_pool.tile([P, GROUP], BF16)
+            nc.sync.dma_start(out=fc_raw[:].rearrange("k (r w) -> k r w", w=2 * P), in_=fc_view[:, i])
+            fc_raws[i] = fc_raw
+
+        def load_fg(child):
+            ci, cj = children[child]
+            fg_raw = fg_pool.tile([P, GROUP], BF16)
             for a in range(2):
                 nc.sync.dma_start(
                     out=fg_raw[:, a * 1024 : (a + 1) * 1024].rearrange("k (r o) -> k r o", o=P),
                     in_=fg_view[:, 2 * ci + a, 8 * cj : 8 * cj + 8, :],
                 )
-            fg_raws[step] = fg_raw
+            fg_raws[child] = fg_raw
 
-        def quantise_weights(raw, codes, scales):
-            grouped = group_pool.tile([P, GROUP], BF16, align_bytes=64, tag="w_grouped")
-            nc.vector.tensor_copy(
+        def regroup(raw, grouped):
+            nc.gpsimd.tensor_scalar(
                 out=grouped[:].rearrange("k (g o t) -> k g o t", g=4, t=PACK),
-                in_=raw[:].rearrange("k (g t o) -> k g o t", g=4, t=PACK),
+                in0=raw[:].rearrange("k (g t o) -> k g o t", g=4, t=PACK),
+                scalar1=1.0,
+                scalar2=0.0,
+                op0=mult,
+                op1=add,
             )
-            nc.vector.quantize_mx(out=codes.bitcast(FP8X4), scales=scales, in_=grouped[:])
 
         fc_codes = const.tile([P, 4, N_COLS], U32, align_bytes=64)
         fc_scales = const.tile([P, 4, N_COLS], U8, align_bytes=64)
 
-        def load_fc(i):
-            fc_raw = raw_pool.tile([P, GROUP], BF16)
-            nc.sync.dma_start(out=fc_raw[:].rearrange("k (r w) -> k r w", w=2 * P), in_=fc_view[:, i])
-            fc_raws[i] = fc_raw
+        def regroup_fc(i):
+            fc_group = fc_pool.tile([P, GROUP], BF16, align_bytes=64)
+            regroup(fc_raws[i], fc_group)
+            fc_groups[i] = fc_group
 
         def quantise_fc(i):
-            quantise_weights(fc_raws[i], fc_codes[:, i, :], fc_scales[:, i, :])
+            nc.vector.quantize_mx(out=fc_codes[:, i, :].bitcast(FP8X4), scales=fc_scales[:, i, :], in_=fc_groups[i][:])
 
-        def quantise_fg(step):
+        def regroup_fg(child):
+            fg_group = group_pool.tile([P, GROUP], BF16, align_bytes=64)
+            regroup(fg_raws[child], fg_group)
+            fg_groups[child] = fg_group
+
+        def quantise_fg(child):
             fg_code = code_pool.tile([P, N_COLS], U32, align_bytes=64)
             fg_scale = code_pool.tile([P, N_COLS], U8, align_bytes=64)
-            quantise_weights(fg_raws[step], fg_code[:], fg_scale[:])
-            fg_codes[step] = (fg_code, fg_scale)
+            nc.vector.quantize_mx(out=fg_code[:].bitcast(FP8X4), scales=fg_scale[:], in_=fg_groups[child][:])
+            fg_codes[child] = (fg_code, fg_scale)
 
-        def new_x_codes(parent):
-            x_code = x_code_pool.tile([P, CHUNKS, N_COLS], U32, align_bytes=64)
-            x_scale = x_code_pool.tile([P, CHUNKS, N_COLS], U8, align_bytes=64)
-            x_codes[parent] = (x_code, x_scale)
-
-        def quantise_patches(parent, chunk):
-            x_words = x_tiles[parent][:].bitcast(F32)
-            x_code, x_scale = x_codes[parent]
+        def flip_patches(parent, chunk):
+            x_words = x_tiles[(parent, chunk)][:].bitcast(F32)
             patches = group_pool.tile([P, GROUP], BF16, align_bytes=64)
             patch_words = patches[:].bitcast(F32).rearrange("k (hi r t) -> k hi r t", hi=2, t=PACK)
             for hi in range(2):
                 flipped = psum_t.tile([P, PACK, P], F32)
                 for x_low in range(2):
                     for p in range(2):
-                        x = 2 * (4 * hi + chunk) + x_low
-                        first = p * (X_ROW // 4) + x * P
+                        first = (2 * p + hi) * 2 * P + x_low * P
                         nc.tensor.transpose(flipped[:, 2 * x_low + p, :], x_words[:, first : first + P], ident_f32[:])
-                nc.scalar.copy(out=patch_words[:, hi], in_=flipped[:].rearrange("k t r -> k r t"))
-            nc.vector.quantize_mx(out=x_code[:, chunk, :].bitcast(FP8X4), scales=x_scale[:, chunk, :], in_=patches[:])
+                nc.vector.tensor_copy(out=patch_words[:, hi], in_=flipped[:].rearrange("k t r -> k r t"))
+            patch_tiles[(parent, chunk)] = patches
 
-        def level_1(step):
-            ci, cj = children[step]
-            x_code, x_scale = x_codes[step // 4]
-            h_bf = group_pool.tile([P, GROUP], BF16, align_bytes=64)
-            for chunk in range(CHUNKS):
-                h_ps = psum_h.tile([P, N_COLS], F32)
-                nc.tensor.matmul_mx(
-                    out=h_ps[:],
-                    lhsT=fc_codes[:, ci, cj * P : (cj + 1) * P].bitcast(FP8X4),
-                    lhsT_scale=fc_scales[:, ci, cj * P : (cj + 1) * P],
-                    rhs=x_code[:, chunk, :].bitcast(FP8X4),
-                    rhs_scale=x_scale[:, chunk, :],
-                    start=True,
-                    stop=True,
-                )
-                nc.scalar.activation(
-                    out=h_bf[:, chunk * N_COLS : (chunk + 1) * N_COLS].rearrange("k (r hi t) -> k r hi t", hi=2, t=PACK),
-                    in_=h_ps[:].rearrange("k (hi r t) -> k r hi t", hi=2, t=PACK),
-                    func=relu,
-                    bias=bias_cols[:, 4 * ci + cj : 4 * ci + cj + 1],
-                    scale=1.0,
-                )
+        def quantise_patches(parent, chunk):
+            if chunk == 0:
+                x_code = x_code_pool.tile([P, CHUNKS, N_COLS], U32, align_bytes=64)
+                x_scale = x_code_pool.tile([P, CHUNKS, N_COLS], U8, align_bytes=64)
+                x_codes[parent] = (x_code, x_scale)
+            x_code, x_scale = x_codes[parent]
+            nc.vector.quantize_mx(
+                out=x_code[:, chunk, :].bitcast(FP8X4),
+                scales=x_scale[:, chunk, :],
+                in_=patch_tiles[(parent, chunk)][:],
+            )
+
+        def level_1_pass(child, chunk):
+            ci, cj = children[child]
+            x_code, x_scale = x_codes[child // 4]
+            if chunk == 0:
+                h_bf = group_pool.tile([P, GROUP], BF16, align_bytes=64)
+                h_tiles[child] = h_bf
+            h_ps = psum_h.tile([P, N_COLS], F32)
+            nc.tensor.matmul_mx(
+                out=h_ps[:],
+                lhsT=fc_codes[:, ci, cj * P : (cj + 1) * P].bitcast(FP8X4),
+                lhsT_scale=fc_scales[:, ci, cj * P : (cj + 1) * P],
+                rhs=x_code[:, chunk, :].bitcast(FP8X4),
+                rhs_scale=x_scale[:, chunk, :],
+                start=True,
+                stop=True,
+            )
+            nc.scalar.activation(
+                out=h_tiles[child][:, chunk * N_COLS : (chunk + 1) * N_COLS].rearrange(
+                    "k (r hi t) -> k r hi t", hi=2, t=PACK
+                ),
+                in_=h_ps[:].rearrange("k (hi r t) -> k r hi t", hi=2, t=PACK),
+                func=relu,
+                bias=bias_cols[:, 4 * ci + cj : 4 * ci + cj + 1],
+                scale=1.0,
+            )
+
+        def quantise_h(child):
             h_code = code_pool.tile([P, N_COLS], U32, align_bytes=64)
             h_scale = code_pool.tile([P, N_COLS], U8, align_bytes=64)
-            nc.vector.quantize_mx(out=h_code[:].bitcast(FP8X4), scales=h_scale[:], in_=h_bf[:])
-            h_codes[step] = (h_code, h_scale)
+            nc.vector.quantize_mx(out=h_code[:].bitcast(FP8X4), scales=h_scale[:], in_=h_tiles[child][:])
+            h_codes[child] = (h_code, h_scale)
 
-        def level_2(step):
-            ci, cj = children[step]
-            h_code, h_scale = h_codes[step]
-            fg_code, fg_scale = fg_codes[step]
-            out_sb = out_pool.tile([P, 4, CHUNKS, P], F32)
-            for chunk in range(CHUNKS):
-                o_ps = psum_o.tile([P, N_COLS], F32)
-                nc.tensor.matmul_mx(
-                    out=o_ps[:],
-                    lhsT=h_code[:, chunk * P : (chunk + 1) * P].bitcast(FP8X4),
-                    lhsT_scale=h_scale[:, chunk * P : (chunk + 1) * P],
-                    rhs=fg_code[:].bitcast(FP8X4),
-                    rhs_scale=fg_scale[:],
-                    start=True,
-                    stop=True,
-                )
-                nc.vector.tensor_tensor(
-                    out=out_sb[:, :, chunk, :].rearrange("k (a e) o -> k a e o", a=2),
-                    in0=o_ps[:].rearrange("k (a e o) -> k a e o", a=2, e=2),
-                    in1=bias_spread[:, 2 * ci : 2 * ci + 2, 2 * cj : 2 * cj + 2, :],
-                    op=add,
-                )
-            flat = out_sb[:].rearrange("k g lo o -> k (g lo o)")
-            nc.scalar.activation(out=flat, in_=flat, func=relu)
+        def level_2_pass(child, chunk):
+            ci, cj = children[child]
+            h_code, h_scale = h_codes[child]
+            fg_code, fg_scale = fg_codes[child]
+            if chunk == 0:
+                out_sb = out_pool.tile([P, 4, CHUNKS, P], F32)
+                out_tiles[child] = out_sb
+            o_ps = psum_o.tile([P, N_COLS], F32)
+            nc.tensor.matmul_mx(
+                out=o_ps[:],
+                lhsT=h_code[:, chunk * P : (chunk + 1) * P].bitcast(FP8X4),
+                lhsT_scale=h_scale[:, chunk * P : (chunk + 1) * P],
+                rhs=fg_code[:].bitcast(FP8X4),
+                rhs_scale=fg_scale[:],
+                start=True,
+                stop=True,
+            )
+            nc.vector.tensor_tensor(
+                out=out_tiles[child][:, :, chunk, :].rearrange("k (a e) o -> k a e o", a=2),
+                in0=o_ps[:].rearrange("k (a e o) -> k a e o", a=2, e=2),
+                in1=bias_spread[:, 2 * ci : 2 * ci + 2, 2 * cj : 2 * cj + 2, :],
+                op=add,
+            )
+
+        def finish(child):
+            ci, cj = children[child]
+            out_sb = out_tiles[child]
             for a in range(2):
-                nc.scalar.dma_start(
-                    out=out_view[2 * ci + a, :, 2 * cj : 2 * cj + 2, :],
-                    in_=out_sb[:, 2 * a : 2 * a + 2, :, :].rearrange("k e lo o -> k e (lo o)"),
-                )
+                pair = out_sb[:, 2 * a : 2 * a + 2, :, :].rearrange("k e lo o -> k e (lo o)")
+                nc.scalar.activation(out=pair, in_=pair, func=relu)
+                nc.sync.dma_start(out=out_view[2 * ci + a, :, 2 * cj : 2 * cj + 2, :], in_=pair)
 
         bias_rows = const.tile([P, P], BF16)
         nc.vector.memset(bias_rows[:], 0.0)
@@ -181,12 +223,6 @@ def tile_butterflylayer2d_pa_kernel(tc, x_parent, f_child, b_child, f_gchild, b_
         nc.sync.dma_start(
             out=bias_rows[CHILDREN : CHILDREN + GRANDCHILDREN, :], in_=b_gchild.rearrange("i j o -> (i j) o")
         )
-        load_fc(0)
-        load_x(0)
-        load_fc(1)
-        load_fg(0)
-        load_fg(1)
-        load_x(1)
 
         ident_bf = const.tile([P, P], BF16)
         make_identity(nc, ident_bf[:])
@@ -200,48 +236,50 @@ def tile_butterflylayer2d_pa_kernel(tc, x_parent, f_child, b_child, f_gchild, b_
         bias_cols_bf = const.tile([P, P], BF16)
         nc.vector.tensor_copy(out=bias_cols_bf[:], in_=bias_ps[:])
         bias_spread = const.tile([P, 8, 8, P], BF16)
-        for i in range(8):
-            for half in range(2):
-                spread_ps = psum_o.tile([P, 4, P], F32, tag="o_ps")
-                for j in range(4):
-                    node = CHILDREN + 8 * i + 4 * half + j
-                    nc.tensor.matmul(
-                        out=spread_ps[:, j, :],
-                        lhsT=bias_cols_bf[:, node : node + 1].to_broadcast([P, P]),
-                        rhs=ident_bf[:],
-                        start=True,
-                        stop=True,
-                    )
-                if half == 0:
-                    nc.vector.tensor_copy(out=bias_spread[:, i, 0:4, :], in_=spread_ps[:])
-                else:
-                    nc.scalar.copy(out=bias_spread[:, i, 4:8, :], in_=spread_ps[:])
 
-        quantise_fc(0)
-        new_x_codes(0)
-        for chunk in range(CHUNKS):
-            quantise_patches(0, chunk)
-        quantise_fc(1)
-        quantise_fg(0)
+        def spread_bias(i):
+            spread_ps = psum_o.tile([P, 8, P], BF16, tag="o_ps")
+            for j in range(8):
+                node = CHILDREN + 8 * i + j
+                nc.tensor.matmul(
+                    out=spread_ps[:, j, :],
+                    lhsT=bias_cols_bf[:, node : node + 1].to_broadcast([P, P]),
+                    rhs=ident_bf[:],
+                    start=True,
+                    stop=True,
+                )
+            nc.scalar.copy(out=bias_spread[:, i, :, :], in_=spread_ps[:])
 
-        for step in range(CHILDREN):
-            parent = step // 4
-            chunk = step % 4
-            if step + 2 < CHILDREN:
-                load_fg(step + 2)
-            if chunk == 0 and parent + 2 < PARENTS:
-                load_x(parent + 2)
-            if step < 2:
-                load_fc(step + 2)
-            elif step < 4:
-                quantise_fc(step)
-            if step + 1 < CHILDREN:
-                quantise_fg(step + 1)
-            if parent + 1 < PARENTS:
-                if chunk == 0:
-                    new_x_codes(parent + 1)
-                quantise_patches(parent + 1, chunk)
-            level_1(step)
-            if step > 0:
-                level_2(step - 1)
-        level_2(CHILDREN - 1)
+        for step in range(-X_LOAD_LEAD, CHILDREN + FINISH_LAG):
+            row, phase = divmod(step + X_LOAD_LEAD, 4)
+            if phase == 0 and live(row, 4):
+                load_fc(row)
+            parent, chunk = divmod(step + X_LOAD_LEAD, CHUNKS)
+            if live(parent, PARENTS):
+                load_x(parent, chunk)
+            if live(step + FG_LOAD_LEAD, CHILDREN):
+                load_fg(step + FG_LOAD_LEAD)
+            for chunk in range(CHUNKS):
+                if live(step, CHILDREN):
+                    level_1_pass(step, chunk)
+                if live(step - LEVEL_2_LAG, CHILDREN):
+                    level_2_pass(step - LEVEL_2_LAG, chunk)
+            if live(step + FLIP_LEAD, 8):
+                spread_bias(step + FLIP_LEAD)
+            parent, chunk = divmod(step + FLIP_LEAD, CHUNKS)
+            if live(parent, PARENTS):
+                flip_patches(parent, chunk)
+            if live(step - 1, CHILDREN):
+                quantise_h(step - 1)
+            if live(parent, PARENTS):
+                quantise_patches(parent, chunk)
+            if phase == 3 and live(row, 4):
+                quantise_fc(row)
+            if live(step, CHILDREN):
+                quantise_fg(step)
+            if phase == 2 and live(row, 4):
+                regroup_fc(row)
+            if live(step + REGROUP_LEAD, CHILDREN):
+                regroup_fg(step + REGROUP_LEAD)
+            if live(step - FINISH_LAG, CHILDREN):
+                finish(step - FINISH_LAG)

@@ -20,10 +20,11 @@ GRANDCHILDREN = 64
 
 X_LOAD_LEAD = 7
 FLIP_LEAD = 4
-LEVEL_2_LAG = 2
-FINISH_LAG = 3
+FINISH_LAG = 2
 FG_LOAD_LEAD = 4
 REGROUP_LEAD = 2
+FC_LOAD_STEP = (-4, -2, 2, 4)
+FC_REGROUP_STEP = (-4, 0, 4, 6)
 
 FLOPS = 2 * 512 * P * (CHILDREN * 2048 + GRANDCHILDREN * 512)
 
@@ -96,8 +97,8 @@ def tile_butterflylayer2d_pa_kernel(tc, x_parent, f_child, b_child, f_gchild, b_
                 )
             fg_raws[child] = fg_raw
 
-        def regroup(raw, grouped):
-            nc.gpsimd.tensor_scalar(
+        def regroup(engine, raw, grouped):
+            engine.tensor_scalar(
                 out=grouped[:].rearrange("k (g o t) -> k g o t", g=4, t=PACK),
                 in0=raw[:].rearrange("k (g t o) -> k g o t", g=4, t=PACK),
                 scalar1=1.0,
@@ -111,7 +112,7 @@ def tile_butterflylayer2d_pa_kernel(tc, x_parent, f_child, b_child, f_gchild, b_
 
         def regroup_fc(i):
             fc_group = fc_pool.tile([P, GROUP], BF16, align_bytes=64)
-            regroup(fc_raws[i], fc_group)
+            regroup(nc.vector, fc_raws[i], fc_group)
             fc_groups[i] = fc_group
 
         def quantise_fc(i):
@@ -119,7 +120,7 @@ def tile_butterflylayer2d_pa_kernel(tc, x_parent, f_child, b_child, f_gchild, b_
 
         def regroup_fg(child):
             fg_group = group_pool.tile([P, GROUP], BF16, align_bytes=64)
-            regroup(fg_raws[child], fg_group)
+            regroup(nc.vector if child < 2 else nc.gpsimd, fg_raws[child], fg_group)
             fg_groups[child] = fg_group
 
         def quantise_fg(child):
@@ -138,7 +139,10 @@ def tile_butterflylayer2d_pa_kernel(tc, x_parent, f_child, b_child, f_gchild, b_
                     for p in range(2):
                         first = (2 * p + hi) * 2 * P + x_low * P
                         nc.tensor.transpose(flipped[:, 2 * x_low + p, :], x_words[:, first : first + P], ident_f32[:])
-                nc.vector.tensor_copy(out=patch_words[:, hi], in_=flipped[:].rearrange("k t r -> k r t"))
+                if hi == 1:
+                    nc.scalar.copy(out=patch_words[:, hi], in_=flipped[:].rearrange("k t r -> k r t"))
+                else:
+                    nc.vector.tensor_copy(out=patch_words[:, hi], in_=flipped[:].rearrange("k t r -> k r t"))
             patch_tiles[(parent, chunk)] = patches
 
         def quantise_patches(parent, chunk):
@@ -217,6 +221,7 @@ def tile_butterflylayer2d_pa_kernel(tc, x_parent, f_child, b_child, f_gchild, b_
                 nc.scalar.activation(out=pair, in_=pair, func=relu)
                 nc.sync.dma_start(out=out_view[2 * ci + a, :, 2 * cj : 2 * cj + 2, :], in_=pair)
 
+        load_x(0, 0)
         bias_rows = const.tile([P, P], BF16)
         nc.vector.memset(bias_rows[:], 0.0)
         nc.sync.dma_start(out=bias_rows[0:CHILDREN, :], in_=b_child.rearrange("i j o -> (i j) o"))
@@ -250,35 +255,41 @@ def tile_butterflylayer2d_pa_kernel(tc, x_parent, f_child, b_child, f_gchild, b_
                 )
             nc.scalar.copy(out=bias_spread[:, i, :, :], in_=spread_ps[:])
 
-        for step in range(-X_LOAD_LEAD, CHILDREN + FINISH_LAG):
-            row, phase = divmod(step + X_LOAD_LEAD, 4)
-            if phase == 0 and live(row, 4):
-                load_fc(row)
+        for step in range(-FLIP_LEAD, CHILDREN + FINISH_LAG):
+            if step in FC_LOAD_STEP:
+                load_fc(FC_LOAD_STEP.index(step))
+            if step == -FLIP_LEAD:
+                for chunk in range(1, CHUNKS):
+                    load_x(0, chunk)
             parent, chunk = divmod(step + X_LOAD_LEAD, CHUNKS)
-            if live(parent, PARENTS):
+            if parent > 0 and live(parent, PARENTS):
                 load_x(parent, chunk)
             if live(step + FG_LOAD_LEAD, CHILDREN):
                 load_fg(step + FG_LOAD_LEAD)
-            for chunk in range(CHUNKS):
-                if live(step, CHILDREN):
+            if live(step, CHILDREN):
+                for chunk in range(3):
                     level_1_pass(step, chunk)
-                if live(step - LEVEL_2_LAG, CHILDREN):
-                    level_2_pass(step - LEVEL_2_LAG, chunk)
-            if live(step + FLIP_LEAD, 8):
-                spread_bias(step + FLIP_LEAD)
+            if live(step - 1, CHILDREN):
+                quantise_h(step - 1)
+            if step - 1 in FC_REGROUP_STEP:
+                quantise_fc(FC_REGROUP_STEP.index(step - 1))
+            if live(step, CHILDREN):
+                quantise_fg(step)
             parent, chunk = divmod(step + FLIP_LEAD, CHUNKS)
             if live(parent, PARENTS):
                 flip_patches(parent, chunk)
+            if live(step, CHILDREN):
+                level_1_pass(step, 3)
             if live(step - 1, CHILDREN):
-                quantise_h(step - 1)
+                for c in range(CHUNKS):
+                    level_2_pass(step - 1, c)
+            if step < 0:
+                spread_bias(2 * (step + FLIP_LEAD))
+                spread_bias(2 * (step + FLIP_LEAD) + 1)
             if live(parent, PARENTS):
                 quantise_patches(parent, chunk)
-            if phase == 3 and live(row, 4):
-                quantise_fc(row)
-            if live(step, CHILDREN):
-                quantise_fg(step)
-            if phase == 2 and live(row, 4):
-                regroup_fc(row)
+            if step in FC_REGROUP_STEP:
+                regroup_fc(FC_REGROUP_STEP.index(step))
             if live(step + REGROUP_LEAD, CHILDREN):
                 regroup_fg(step + REGROUP_LEAD)
             if live(step - FINISH_LAG, CHILDREN):

@@ -19,6 +19,8 @@ CHILDREN = 16
 GRANDCHILDREN = 64
 
 X_LOAD_LEAD = 7
+X_MAP_LEAD = 2
+X_CHUNKS = (1, 2, 4, 4)
 FLIP_LEAD = 4
 FINISH_LAG = 2
 FG_LOAD_LEAD = 4
@@ -39,7 +41,11 @@ def tile_butterflylayer2d_pa_kernel(tc, x_parent, f_child, b_child, f_gchild, b_
     add = mybir.AluOpType.add
     mult = mybir.AluOpType.mult
 
-    x_view = x_parent.rearrange("u v n (y p) (hi lo w) c -> (u v) lo (n y) (p hi) (w c)", p=2, hi=2, lo=CHUNKS)
+    def x_view(chunks):
+        return x_parent.rearrange(
+            "u v n (y p) (hi lo w) c -> (u v) lo (n y) (p hi) (w c)", p=2, hi=2, lo=CHUNKS // chunks
+        )
+
     fc_view = f_child.rearrange("i j p q (cw e) o -> (q cw) i (j p) (e o)", e=2)
     fg_view = f_gchild.rearrange("i j p q c o -> c i (j p q) o")
     out_view = out.rearrange("i j n y (hi lo) o -> i (n y hi) j (lo o)", hi=2)
@@ -53,7 +59,8 @@ def tile_butterflylayer2d_pa_kernel(tc, x_parent, f_child, b_child, f_gchild, b_
 
     with ExitStack() as ctx:
         const = ctx.enter_context(tc.tile_pool(name="const", bufs=1))
-        x_pool = ctx.enter_context(tc.tile_pool(name="x", bufs=5))
+        x_pool = ctx.enter_context(tc.tile_pool(name="x", bufs=4))
+        x_map_pool = ctx.enter_context(tc.tile_pool(name="xmap", bufs=2))
         fc_pool = ctx.enter_context(tc.tile_pool(name="fc", bufs=4))
         fg_pool = ctx.enter_context(tc.tile_pool(name="fg", bufs=6))
         group_pool = ctx.enter_context(tc.tile_pool(name="group", bufs=2))
@@ -66,6 +73,7 @@ def tile_butterflylayer2d_pa_kernel(tc, x_parent, f_child, b_child, f_gchild, b_
         ctx.enter_context(tc.manual_schedule())
 
         x_tiles = {}
+        x_words = {}
         x_codes = {}
         patch_tiles = {}
         fc_raws = {}
@@ -78,9 +86,18 @@ def tile_butterflylayer2d_pa_kernel(tc, x_parent, f_child, b_child, f_gchild, b_
         out_tiles = {}
 
         def load_x(parent, chunk):
-            x_sb = x_pool.tile([P, GROUP], BF16)
-            nc.sync.dma_start(out=x_sb[:].rearrange("k (s r) -> k s r", s=PACK), in_=x_view[parent, chunk])
-            x_tiles[(parent, chunk)] = x_sb
+            chunks = X_CHUNKS[parent]
+            if chunk % chunks == 0:
+                x_sb = (x_pool if chunks == 1 else x_map_pool).tile([P, chunks * GROUP], BF16, tag="x%d" % chunks)
+                for c in range(chunks):
+                    words = x_sb[:].bitcast(F32).rearrange("k (p hi lo xl r) -> k lo p hi xl r", p=2, hi=2, xl=2, r=P)
+                    x_words[(parent, chunk + c)] = words[:, c]
+                x_tiles[parent] = x_sb
+            x_runs = x_tiles[parent][:].rearrange("k (s r) -> k s r", s=PACK)
+            if chunks == CHUNKS:
+                nc.sync.dma_start(out=x_runs[:, chunk], in_=x_view(chunks)[parent, 0][:, chunk])
+            elif chunk % chunks == 0:
+                nc.sync.dma_start(out=x_runs, in_=x_view(chunks)[parent, chunk // chunks])
 
         def load_fc(i):
             fc_raw = fc_pool.tile([P, GROUP], BF16)
@@ -130,15 +147,15 @@ def tile_butterflylayer2d_pa_kernel(tc, x_parent, f_child, b_child, f_gchild, b_
             fg_codes[child] = (fg_code, fg_scale)
 
         def flip_patches(parent, chunk):
-            x_words = x_tiles[(parent, chunk)][:].bitcast(F32)
             patches = group_pool.tile([P, GROUP], BF16, align_bytes=64)
             patch_words = patches[:].bitcast(F32).rearrange("k (hi r t) -> k hi r t", hi=2, t=PACK)
             for hi in range(2):
                 flipped = psum_t.tile([P, PACK, P], F32)
                 for x_low in range(2):
                     for p in range(2):
-                        first = (2 * p + hi) * 2 * P + x_low * P
-                        nc.tensor.transpose(flipped[:, 2 * x_low + p, :], x_words[:, first : first + P], ident_f32[:])
+                        nc.tensor.transpose(
+                            flipped[:, 2 * x_low + p, :], x_words[(parent, chunk)][:, p, hi, x_low, :], ident_f32[:]
+                        )
                 if hi == 1:
                     nc.scalar.copy(out=patch_words[:, hi], in_=flipped[:].rearrange("k t r -> k r t"))
                 else:
@@ -196,7 +213,7 @@ def tile_butterflylayer2d_pa_kernel(tc, x_parent, f_child, b_child, f_gchild, b_
             if chunk == 0:
                 out_sb = out_pool.tile([P, 4, CHUNKS, P], F32)
                 out_tiles[child] = out_sb
-            o_ps = psum_o.tile([P, N_COLS], F32)
+            o_ps = psum_o.tile([P, N_COLS], F32, tag="o_ps")
             nc.tensor.matmul_mx(
                 out=o_ps[:],
                 lhsT=h_code[:, chunk * P : (chunk + 1) * P].bitcast(FP8X4),
@@ -220,6 +237,34 @@ def tile_butterflylayer2d_pa_kernel(tc, x_parent, f_child, b_child, f_gchild, b_
                 pair = out_sb[:, 2 * a : 2 * a + 2, :, :].rearrange("k e lo o -> k e (lo o)")
                 nc.scalar.activation(out=pair, in_=pair, func=relu)
                 nc.sync.dma_start(out=out_view[2 * ci + a, :, 2 * cj : 2 * cj + 2, :], in_=pair)
+
+        def last_child():
+            child = CHILDREN - 1
+            ci, cj = children[child]
+            h_code, h_scale = h_codes[child]
+            fg_code, fg_scale = fg_codes[child]
+            out_sb = out_pool.tile([P, 4, CHUNKS, P], F32)
+            for g in range(4):
+                i, j = 2 * ci + g // 2, 2 * cj + g % 2
+                o_ps = psum_o.tile([P, CHUNKS, P], F32, tag="o_ps")
+                for chunk in range(CHUNKS):
+                    nc.tensor.matmul_mx(
+                        out=o_ps[:, chunk, :],
+                        lhsT=h_code[:, chunk * P : (chunk + 1) * P].bitcast(FP8X4),
+                        lhsT_scale=h_scale[:, chunk * P : (chunk + 1) * P],
+                        rhs=fg_code[:, g * P : (g + 1) * P].bitcast(FP8X4),
+                        rhs_scale=fg_scale[:, g * P : (g + 1) * P],
+                        start=True,
+                        stop=True,
+                    )
+                nc.vector.tensor_tensor(
+                    out=out_sb[:, g],
+                    in0=o_ps[:],
+                    in1=bias_spread[:, i, j, :].unsqueeze(1).to_broadcast([P, CHUNKS, P]),
+                    op=add,
+                )
+                nc.scalar.activation(out=out_sb[:, g], in_=out_sb[:, g], func=relu)
+                nc.sync.dma_start(out=out_view[i, :, j, :], in_=out_sb[:, g].rearrange("k lo o -> k (lo o)"))
 
         load_x(0, 0)
         bias_rows = const.tile([P, P], BF16)
@@ -255,14 +300,17 @@ def tile_butterflylayer2d_pa_kernel(tc, x_parent, f_child, b_child, f_gchild, b_
                 )
             nc.scalar.copy(out=bias_spread[:, i, :, :], in_=spread_ps[:])
 
-        for step in range(-FLIP_LEAD, CHILDREN + FINISH_LAG):
+        for step in range(-FLIP_LEAD, CHILDREN + 1):
             if step in FC_LOAD_STEP:
                 load_fc(FC_LOAD_STEP.index(step))
             if step == -FLIP_LEAD:
                 for chunk in range(1, CHUNKS):
                     load_x(0, chunk)
             parent, chunk = divmod(step + X_LOAD_LEAD, CHUNKS)
-            if parent > 0 and live(parent, PARENTS):
+            if parent == 1:
+                load_x(parent, chunk)
+            parent, chunk = divmod(step + X_LOAD_LEAD + X_MAP_LEAD, CHUNKS)
+            if 2 <= parent < PARENTS:
                 load_x(parent, chunk)
             if live(step + FG_LOAD_LEAD, CHILDREN):
                 load_fg(step + FG_LOAD_LEAD)
@@ -280,9 +328,12 @@ def tile_butterflylayer2d_pa_kernel(tc, x_parent, f_child, b_child, f_gchild, b_
                 flip_patches(parent, chunk)
             if live(step, CHILDREN):
                 level_1_pass(step, 3)
-            if live(step - 1, CHILDREN):
+            if live(step - 1, CHILDREN - 1):
                 for c in range(CHUNKS):
                     level_2_pass(step - 1, c)
+            if step == CHILDREN:
+                finish(step - FINISH_LAG)
+                last_child()
             if step < 0:
                 spread_bias(2 * (step + FLIP_LEAD))
                 spread_bias(2 * (step + FLIP_LEAD) + 1)
@@ -292,5 +343,5 @@ def tile_butterflylayer2d_pa_kernel(tc, x_parent, f_child, b_child, f_gchild, b_
                 regroup_fc(FC_REGROUP_STEP.index(step))
             if live(step + REGROUP_LEAD, CHILDREN):
                 regroup_fg(step + REGROUP_LEAD)
-            if live(step - FINISH_LAG, CHILDREN):
+            if live(step - FINISH_LAG, CHILDREN - FINISH_LAG):
                 finish(step - FINISH_LAG)

@@ -114,22 +114,22 @@ def tile_butterflylayer2d_pa_kernel(tc, x_parent, f_child, b_child, f_gchild, b_
                 )
             fg_raws[child] = fg_raw
 
-        def regroup(engine, raw, grouped):
-            engine.tensor_scalar(
-                out=grouped[:].rearrange("k (g o t) -> k g o t", g=4, t=PACK),
-                in0=raw[:].rearrange("k (g t o) -> k g o t", g=4, t=PACK),
-                scalar1=1.0,
-                scalar2=0.0,
-                op0=mult,
-                op1=add,
-            )
+        def regroup(on_vector, raw, grouped):
+            grouped_view = grouped[:].rearrange("k (g o t) -> k g o t", g=4, t=PACK)
+            raw_view = raw[:].rearrange("k (g t o) -> k g o t", g=4, t=PACK)
+            if on_vector:
+                nc.vector.tensor_copy(out=grouped_view, in_=raw_view)
+            else:
+                nc.gpsimd.tensor_scalar(
+                    out=grouped_view, in0=raw_view, scalar1=1.0, scalar2=0.0, op0=mult, op1=add
+                )
 
         fc_codes = const.tile([P, 4, N_COLS], U32, align_bytes=64)
         fc_scales = const.tile([P, 4, N_COLS], U8, align_bytes=64)
 
         def regroup_fc(i):
             fc_group = fc_pool.tile([P, GROUP], BF16, align_bytes=64)
-            regroup(nc.vector, fc_raws[i], fc_group)
+            regroup(True, fc_raws[i], fc_group)
             fc_groups[i] = fc_group
 
         def quantise_fc(i):
@@ -137,7 +137,7 @@ def tile_butterflylayer2d_pa_kernel(tc, x_parent, f_child, b_child, f_gchild, b_
 
         def regroup_fg(child):
             fg_group = group_pool.tile([P, GROUP], BF16, align_bytes=64)
-            regroup(nc.vector if child < 2 else nc.gpsimd, fg_raws[child], fg_group)
+            regroup(child < 2, fg_raws[child], fg_group)
             fg_groups[child] = fg_group
 
         def quantise_fg(child):

from contextlib import ExitStack

import concourse.mybir as mybir
from concourse.masks import make_identity

F32 = mybir.dt.float32
BF16 = mybir.dt.bfloat16
U32 = mybir.dt.uint32
U8 = mybir.dt.uint8
FP8X4 = mybir.dt.float8_e4m3fn_x4

P = 128
PACK = 4
N_COLS = 512
GROUP = PACK * N_COLS
CHUNKS = 4
PARENTS = 4
CHILDREN = 16
GRANDCHILDREN = 64

X_LOAD_LEAD = 7
X_MAP_LEAD = 2
X_CHUNKS = (1, 2, 4, 4)
FLIP_LEAD = 4
FINISH_LAG = 2
FG_LOAD_LEAD = 4
REGROUP_LEAD = 2
FC_LOAD_STEP = (-4, -2, 2, 4)
FC_REGROUP_STEP = (-4, 0, 4, 6)

FLOPS = 2 * 512 * P * (CHILDREN * 2048 + GRANDCHILDREN * 512)


def live(index, count):
    return 0 <= index < count


def tile_butterflylayer2d_pa_kernel(tc, x_parent, f_child, b_child, f_gchild, b_gchild, out):
    nc = tc.nc
    relu = mybir.ActivationFunctionType.Relu
    add = mybir.AluOpType.add
    mult = mybir.AluOpType.mult

    def x_view(chunks):
        return x_parent.rearrange(
            "u v n (y p) (hi lo w) c -> (u v) lo (n y) (p hi) (w c)", p=2, hi=2, lo=CHUNKS // chunks
        )

    fc_view = f_child.rearrange("i j p q (cw e) o -> (q cw) i (j p) (e o)", e=2)
    fg_view = f_gchild.rearrange("i j p q c o -> c i (j p q) o")
    out_view = out.rearrange("i j n y (hi lo) o -> i (n y hi) j (lo o)", hi=2)

    children = []
    for u in range(2):
        for v in range(2):
            for a in range(2):
                for e in range(2):
                    children.append((2 * u + a, 2 * v + e))

    with ExitStack() as ctx:
        const = ctx.enter_context(tc.tile_pool(name="const", bufs=1))
        x_pool = ctx.enter_context(tc.tile_pool(name="x", bufs=4))
        x_map_pool = ctx.enter_context(tc.tile_pool(name="xmap", bufs=2))
        fc_pool = ctx.enter_context(tc.tile_pool(name="fc", bufs=4))
        fg_pool = ctx.enter_context(tc.tile_pool(name="fg", bufs=6))
        group_pool = ctx.enter_context(tc.tile_pool(name="group", bufs=2))
        x_code_pool = ctx.enter_context(tc.tile_pool(name="xcode", bufs=2))
        code_pool = ctx.enter_context(tc.tile_pool(name="code", bufs=3))
        out_pool = ctx.enter_context(tc.tile_pool(name="outs", bufs=4))
        psum_t = ctx.enter_context(tc.psum_pool(name="psum_t", bufs=2))
        psum_h = ctx.enter_context(tc.psum_pool(name="psum_h", bufs=3))
        psum_o = ctx.enter_context(tc.psum_pool(name="psum_o", bufs=3))
        ctx.enter_context(tc.manual_schedule())

        x_tiles = {}
        x_words = {}
        x_codes = {}
        patch_tiles = {}
        fc_raws = {}
        fc_groups = {}
        fg_raws = {}
        fg_groups = {}
        fg_codes = {}
        h_tiles = {}
        h_codes = {}
        out_tiles = {}

        def load_x(parent, chunk):
            chunks = X_CHUNKS[parent]
            if chunk % chunks == 0:
                x_sb = (x_pool if chunks == 1 else x_map_pool).tile([P, chunks * GROUP], BF16, tag="x%d" % chunks)
                for c in range(chunks):
                    words = x_sb[:].bitcast(F32).rearrange("k (p hi lo xl r) -> k lo p hi xl r", p=2, hi=2, xl=2, r=P)
                    x_words[(parent, chunk + c)] = words[:, c]
                x_tiles[parent] = x_sb
            x_runs = x_tiles[parent][:].rearrange("k (s r) -> k s r", s=PACK)
            if chunks == CHUNKS:
                nc.sync.dma_start(out=x_runs[:, chunk], in_=x_view(chunks)[parent, 0][:, chunk])
            elif chunk % chunks == 0:
                nc.sync.dma_start(out=x_runs, in_=x_view(chunks)[parent, chunk // chunks])

        def load_fc(i):
            fc_raw = fc_pool.tile([P, GROUP], BF16)
            nc.sync.dma_start(out=fc_raw[:].rearrange("k (r w) -> k r w", w=2 * P), in_=fc_view[:, i])
            fc_raws[i] = fc_raw

        def load_fg(child):
            ci, cj = children[child]
            fg_raw = fg_pool.tile([P, GROUP], BF16)
            for a in range(2):
                nc.sync.dma_start(
                    out=fg_raw[:, a * 1024 : (a + 1) * 1024].rearrange("k (r o) -> k r o", o=P),
                    in_=fg_view[:, 2 * ci + a, 8 * cj : 8 * cj + 8, :],
                )
            fg_raws[child] = fg_raw

        def regroup(on_vector, raw, grouped):
            grouped_view = grouped[:].rearrange("k (g o t) -> k g o t", g=4, t=PACK)
            raw_view = raw[:].rearrange("k (g t o) -> k g o t", g=4, t=PACK)
            if on_vector:
                nc.vector.tensor_copy(out=grouped_view, in_=raw_view)
            else:
                nc.gpsimd.tensor_scalar(
                    out=grouped_view, in0=raw_view, scalar1=1.0, scalar2=0.0, op0=mult, op1=add
                )

        fc_codes = const.tile([P, 4, N_COLS], U32, align_bytes=64)
        fc_scales = const.tile([P, 4, N_COLS], U8, align_bytes=64)

        def regroup_fc(i):
            fc_group = fc_pool.tile([P, GROUP], BF16, align_bytes=64)
            regroup(True, fc_raws[i], fc_group)
            fc_groups[i] = fc_group

        def quantise_fc(i):
            nc.vector.quantize_mx(out=fc_codes[:, i, :].bitcast(FP8X4), scales=fc_scales[:, i, :], in_=fc_groups[i][:])

        def regroup_fg(child):
            fg_group = group_pool.tile([P, GROUP], BF16, align_bytes=64)
            regroup(child < 2, fg_raws[child], fg_group)
            fg_groups[child] = fg_group

        def quantise_fg(child):
            fg_code = code_pool.tile([P, N_COLS], U32, align_bytes=64)
            fg_scale = code_pool.tile([P, N_COLS], U8, align_bytes=64)
            nc.vector.quantize_mx(out=fg_code[:].bitcast(FP8X4), scales=fg_scale[:], in_=fg_groups[child][:])
            fg_codes[child] = (fg_code, fg_scale)

        def flip_patches(parent, chunk):
            patches = group_pool.tile([P, GROUP], BF16, align_bytes=64)
            patch_words = patches[:].bitcast(F32).rearrange("k (hi r t) -> k hi r t", hi=2, t=PACK)
            for hi in range(2):
                flipped = psum_t.tile([P, PACK, P], F32)
                for x_low in range(2):
                    for p in range(2):
                        nc.tensor.transpose(
                            flipped[:, 2 * x_low + p, :], x_words[(parent, chunk)][:, p, hi, x_low, :], ident_f32[:]
                        )
                if hi == 1:
                    nc.scalar.copy(out=patch_words[:, hi], in_=flipped[:].rearrange("k t r -> k r t"))
                else:
                    nc.vector.tensor_copy(out=patch_words[:, hi], in_=flipped[:].rearrange("k t r -> k r t"))
            patch_tiles[(parent, chunk)] = patches

        def quantise_patches(parent, chunk):
            if chunk == 0:
                x_code = x_code_pool.tile([P, CHUNKS, N_COLS], U32, align_bytes=64)
                x_scale = x_code_pool.tile([P, CHUNKS, N_COLS], U8, align_bytes=64)
                x_codes[parent] = (x_code, x_scale)
            x_code, x_scale = x_codes[parent]
            nc.vector.quantize_mx(
                out=x_code[:, chunk, :].bitcast(FP8X4),
                scales=x_scale[:, chunk, :],
                in_=patch_tiles[(parent, chunk)][:],
            )

        def level_1_pass(child, chunk):
            ci, cj = children[child]
            x_code, x_scale = x_codes[child // 4]
            if chunk == 0:
                h_bf = group_pool.tile([P, GROUP], BF16, align_bytes=64)
                h_tiles[child] = h_bf
            h_ps = psum_h.tile([P, N_COLS], F32)
            nc.tensor.matmul_mx(
                out=h_ps[:],
                lhsT=fc_codes[:, ci, cj * P : (cj + 1) * P].bitcast(FP8X4),
                lhsT_scale=fc_scales[:, ci, cj * P : (cj + 1) * P],
                rhs=x_code[:, chunk, :].bitcast(FP8X4),
                rhs_scale=x_scale[:, chunk, :],
                start=True,
                stop=True,
            )
            nc.scalar.activation(
                out=h_tiles[child][:, chunk * N_COLS : (chunk + 1) * N_COLS].rearrange(
                    "k (r hi t) -> k r hi t", hi=2, t=PACK
                ),
                in_=h_ps[:].rearrange("k (hi r t) -> k r hi t", hi=2, t=PACK),
                func=relu,
                bias=bias_cols[:, 4 * ci + cj : 4 * ci + cj + 1],
                scale=1.0,
            )

        def quantise_h(child):
            h_code = code_pool.tile([P, N_COLS], U32, align_bytes=64)
            h_scale = code_pool.tile([P, N_COLS], U8, align_bytes=64)
            nc.vector.quantize_mx(out=h_code[:].bitcast(FP8X4), scales=h_scale[:], in_=h_tiles[child][:])
            h_codes[child] = (h_code, h_scale)

        def level_2_pass(child, chunk):
            ci, cj = children[child]
            h_code, h_scale = h_codes[child]
            fg_code, fg_scale = fg_codes[child]
            if chunk == 0:
                out_sb = out_pool.tile([P, 4, CHUNKS, P], F32)
                out_tiles[child] = out_sb
            o_ps = psum_o.tile([P, N_COLS], F32, tag="o_ps")
            nc.tensor.matmul_mx(
                out=o_ps[:],
                lhsT=h_code[:, chunk * P : (chunk + 1) * P].bitcast(FP8X4),
                lhsT_scale=h_scale[:, chunk * P : (chunk + 1) * P],
                rhs=fg_code[:].bitcast(FP8X4),
                rhs_scale=fg_scale[:],
                start=True,
                stop=True,
            )
            nc.vector.tensor_tensor(
                out=out_tiles[child][:, :, chunk, :].rearrange("k (a e) o -> k a e o", a=2),
                in0=o_ps[:].rearrange("k (a e o) -> k a e o", a=2, e=2),
                in1=bias_spread[:, 2 * ci : 2 * ci + 2, 2 * cj : 2 * cj + 2, :],
                op=add,
            )

        def finish(child):
            ci, cj = children[child]
            out_sb = out_tiles[child]
            for a in range(2):
                pair = out_sb[:, 2 * a : 2 * a + 2, :, :].rearrange("k e lo o -> k e (lo o)")
                nc.scalar.activation(out=pair, in_=pair, func=relu)
                nc.sync.dma_start(out=out_view[2 * ci + a, :, 2 * cj : 2 * cj + 2, :], in_=pair)

        def last_child():
            child = CHILDREN - 1
            ci, cj = children[child]
            h_code, h_scale = h_codes[child]
            fg_code, fg_scale = fg_codes[child]
            out_sb = out_pool.tile([P, 4, CHUNKS, P], F32)
            for g in range(4):
                i, j = 2 * ci + g // 2, 2 * cj + g % 2
                o_ps = psum_o.tile([P, CHUNKS, P], F32, tag="o_ps")
                for chunk in range(CHUNKS):
                    nc.tensor.matmul_mx(
                        out=o_ps[:, chunk, :],
                        lhsT=h_code[:, chunk * P : (chunk + 1) * P].bitcast(FP8X4),
                        lhsT_scale=h_scale[:, chunk * P : (chunk + 1) * P],
                        rhs=fg_code[:, g * P : (g + 1) * P].bitcast(FP8X4),
                        rhs_scale=fg_scale[:, g * P : (g + 1) * P],
                        start=True,
                        stop=True,
                    )
                nc.vector.tensor_tensor(
                    out=out_sb[:, g],
                    in0=o_ps[:],
                    in1=bias_spread[:, i, j, :].unsqueeze(1).to_broadcast([P, CHUNKS, P]),
                    op=add,
                )
                nc.scalar.activation(out=out_sb[:, g], in_=out_sb[:, g], func=relu)
                nc.sync.dma_start(out=out_view[i, :, j, :], in_=out_sb[:, g].rearrange("k lo o -> k (lo o)"))

        load_x(0, 0)
        bias_rows = const.tile([P, P], BF16)
        nc.vector.memset(bias_rows[:], 0.0)
        nc.sync.dma_start(out=bias_rows[0:CHILDREN, :], in_=b_child.rearrange("i j o -> (i j) o"))
        nc.sync.dma_start(
            out=bias_rows[CHILDREN : CHILDREN + GRANDCHILDREN, :], in_=b_gchild.rearrange("i j o -> (i j) o")
        )

        ident_bf = const.tile([P, P], BF16)
        make_identity(nc, ident_bf[:])
        ident_f32 = const.tile([P, P], F32)
        make_identity(nc, ident_f32[:])

        bias_ps = psum_t.tile([P, P], BF16, tag="flipped")
        nc.tensor.transpose(bias_ps[:], bias_rows[:], ident_bf[:])
        bias_cols = const.tile([P, P], F32)
        nc.vector.tensor_copy(out=bias_cols[:], in_=bias_ps[:])
        bias_cols_bf = const.tile([P, P], BF16)
        nc.vector.tensor_copy(out=bias_cols_bf[:], in_=bias_ps[:])
        bias_spread = const.tile([P, 8, 8, P], BF16)

        def spread_bias(i):
            spread_ps = psum_o.tile([P, 8, P], BF16, tag="o_ps")
            for j in range(8):
                node = CHILDREN + 8 * i + j
                nc.tensor.matmul(
                    out=spread_ps[:, j, :],
                    lhsT=bias_cols_bf[:, node : node + 1].to_broadcast([P, P]),
                    rhs=ident_bf[:],
                    start=True,
                    stop=True,
                )
            nc.scalar.copy(out=bias_spread[:, i, :, :], in_=spread_ps[:])

        for step in range(-FLIP_LEAD, CHILDREN + 1):
            if step in FC_LOAD_STEP:
                load_fc(FC_LOAD_STEP.index(step))
            if step == -FLIP_LEAD:
                for chunk in range(1, CHUNKS):
                    load_x(0, chunk)
            parent, chunk = divmod(step + X_LOAD_LEAD, CHUNKS)
            if parent == 1:
                load_x(parent, chunk)
            parent, chunk = divmod(step + X_LOAD_LEAD + X_MAP_LEAD, CHUNKS)
            if 2 <= parent < PARENTS:
                load_x(parent, chunk)
            if live(step + FG_LOAD_LEAD, CHILDREN):
                load_fg(step + FG_LOAD_LEAD)
            if live(step, CHILDREN):
                for chunk in range(3):
                    level_1_pass(step, chunk)
            if live(step - 1, CHILDREN):
                quantise_h(step - 1)
            if step - 1 in FC_REGROUP_STEP:
                quantise_fc(FC_REGROUP_STEP.index(step - 1))
            if live(step, CHILDREN):
                quantise_fg(step)
            parent, chunk = divmod(step + FLIP_LEAD, CHUNKS)
            if live(parent, PARENTS):
                flip_patches(parent, chunk)
            if live(step, CHILDREN):
                level_1_pass(step, 3)
            if live(step - 1, CHILDREN - 1):
                for c in range(CHUNKS):
                    level_2_pass(step - 1, c)
            if step == CHILDREN:
                finish(step - FINISH_LAG)
                last_child()
            if step < 0:
                spread_bias(2 * (step + FLIP_LEAD))
                spread_bias(2 * (step + FLIP_LEAD) + 1)
            if live(parent, PARENTS):
                quantise_patches(parent, chunk)
            if step in FC_REGROUP_STEP:
                regroup_fc(FC_REGROUP_STEP.index(step))
            if live(step + REGROUP_LEAD, CHILDREN):
                regroup_fg(step + REGROUP_LEAD)
            if live(step - FINISH_LAG, CHILDREN - FINISH_LAG):
                finish(step - FINISH_LAG)
